import numpy as np
import ml_dtypes


def mxq(x, axis, fmt="e4m3"):
    dtype, down = {"e4m3": (ml_dtypes.float8_e4m3fn, 7), "e5m2": (ml_dtypes.float8_e5m2, 14)}[fmt]
    v = np.moveaxis(np.asarray(x, np.float32).astype(ml_dtypes.bfloat16).astype(np.float64), axis, -1)
    blocks = v.reshape(v.shape[:-1] + (-1, 32))
    amax = np.abs(blocks).max(-1, keepdims=True)
    byte = np.maximum(np.where(amax > 0, np.frexp(amax)[1] - 1 + 127, 0) - down, 1)
    scale = np.exp2(byte - 127.0)
    codes = (blocks / scale).astype(np.float32).astype(dtype).astype(np.float64)
    return np.moveaxis((codes * scale).reshape(v.shape), -1, axis)


WIDE = False


def mx_kscale(k):
    if not WIDE:
        return np.ones(k)
    levels = np.array([10, -10, 5, -5, 0])
    if k % 512:
        return np.exp2(np.random.permutation(np.resize(levels, k // 32))).repeat(32)
    a = np.empty((k // 512, 16))
    for p in range(k // 512):
        a[p, :8] = np.random.permutation(np.resize(levels, 8))
        for g in range(8):
            far = levels[np.abs(levels - a[p, g]) >= 10]
            a[p, g + 8] = far[np.random.randint(len(far))]
    return np.exp2(a.ravel()).repeat(32)


BF16 = ml_dtypes.bfloat16


def bf(x):
    return np.asarray(x, np.float32).astype(BF16)


def f64(x):
    return np.asarray(x).astype(np.float64)


B, Q, S, D = 4, 256, 512, 1024
K = D + D


def sigmoid(v):
    return 1.0 / (1.0 + np.exp(-v))


def setup_inputs():
    t = mx_kscale(D)
    s = np.concatenate([np.ones(D), t])
    return {"query": bf(np.random.standard_normal((B, Q, D)) * 0.25),
            "weighted_ctx": bf(np.random.standard_normal((B, Q, D)) * 0.12 * t),
            "W_lin": bf(np.random.standard_normal((K, D)) * 5.0 / np.sqrt(K) / s[:, None]),
            "b_lin": bf(np.random.standard_normal(D) * 0.3),
            "W_gate": bf(np.random.standard_normal((K, D)) * 5.0 / np.sqrt(K) / s[:, None]),
            "b_gate": bf(np.random.standard_normal(D) * 0.3)}


def reference(query, weighted_ctx, W_lin, b_lin, W_gate, b_gate):
    q = f64(query)
    cat = mxq(np.concatenate([q, f64(weighted_ctx)], axis=2), 2, "e4m3")
    h = np.tanh((cat @ mxq(f64(W_lin), 0, "e4m3")) + f64(b_lin))
    g = sigmoid((cat @ mxq(f64(W_gate), 0, "e4m3")) + f64(b_gate))
    return q * g + h * (1.0 - g)

@@ -1,0 +1,259 @@
+from contextlib import ExitStack
+
+import concourse.masks as masks
+import concourse.mybir as mybir
+
+FP8X4 = mybir.dt.float8_e4m3fn_x4
+BF16 = mybir.dt.bfloat16
+F32 = mybir.dt.float32
+U32 = mybir.dt.uint32
+U8 = mybir.dt.uint8
+ACT = mybir.ActivationFunctionType
+ALU = mybir.AluOpType
+
+P = 128
+PACK = 4
+K_PASS = P * PACK
+TOKENS = 1024
+FEATURES = 1024
+PASSES = 2 * FEATURES // K_PASS
+QUERY_PASSES = FEATURES // K_PASS
+TOKEN_TILES = TOKENS // P
+HALF = 512
+HALVES = TOKENS // HALF
+TILES_PER_HALF = HALF // P
+BLOCK = 512
+BLOCKS = FEATURES // BLOCK
+SLICES = BLOCK // P
+STEPS = 2 * BLOCKS
+EARLY_STEPS = 2
+
+FLOPS = 2 * TOKENS * 2 * FEATURES * 2 * FEATURES
+
+
+def tile_smcmr_pb_kernel(tc, query, weighted_ctx, W_lin, b_lin, W_gate, b_gate, out):
+    nc = tc.nc
+    q_dram = query.flatten_outer_dims().rearrange("(p i) d -> p i d", i=TOKEN_TILES)
+    c_dram = weighted_ctx.flatten_outer_dims().rearrange("(p i) d -> p i d", i=TOKEN_TILES)
+    out_dram = out.flatten_outer_dims().rearrange("(p i) d -> p i d", i=TOKEN_TILES)
+
+    with ExitStack() as ctx:
+        keep = ctx.enter_context(tc.tile_pool(name="keep", bufs=1))
+        raw_pool = ctx.enter_context(tc.tile_pool(name="raw", bufs=3))
+        grouped_pool = ctx.enter_context(tc.tile_pool(name="grouped", bufs=2))
+        weight_pool = ctx.enter_context(tc.tile_pool(name="weights", bufs=2))
+        hidden_pool = ctx.enter_context(tc.tile_pool(name="hidden", bufs=3))
+        gate_pool = ctx.enter_context(tc.tile_pool(name="gate", bufs=2))
+        result_pool = ctx.enter_context(tc.tile_pool(name="result", bufs=4))
+        acc_pool = ctx.enter_context(tc.psum_pool(name="acc", bufs=4))
+        flip_pool = ctx.enter_context(tc.psum_pool(name="flip", bufs=4))
+
+        ident_f32 = keep.tile([P, P], F32)
+        masks.make_identity(nc, ident_f32[:])
+
+        warm_in = keep.tile([P, 1], F32)
+        warm_out = keep.tile([P, 1], F32)
+        nc.vector.memset(warm_in[:], 0.0)
+        nc.scalar.activation(out=warm_out[:], in_=warm_in[:], func=ACT.Sigmoid)
+
+        bias_rows = keep.tile([P, BLOCK], BF16)
+        nc.vector.memset(bias_rows[:], 0.0)
+        nc.scalar.dma_start(out=bias_rows[0:BLOCKS, :], in_=b_lin.rearrange("(b n) -> b n", n=BLOCK))
+        nc.scalar.dma_start(out=bias_rows[BLOCKS : 2 * BLOCKS, :], in_=b_gate.rearrange("(b n) -> b n", n=BLOCK))
+
+        q_sb = keep.tile([P, TOKEN_TILES * FEATURES], BF16)
+        q_tiles = q_sb[:].rearrange("p (i d) -> p i d", i=TOKEN_TILES)
+        c_sb = keep.tile([P, TOKEN_TILES * FEATURES], BF16)
+        c_tiles = c_sb[:].rearrange("p (i d) -> p i d", i=TOKEN_TILES)
+        words = [q_sb[:].bitcast(F32), c_sb[:].bitcast(F32)]
+
+        def load_tokens(half):
+            tiles = slice(half * TILES_PER_HALF, (half + 1) * TILES_PER_HALF)
+            nc.sync.dma_start(out=q_tiles[:, tiles, :], in_=q_dram[:, tiles, :])
+            nc.sync.dma_start(out=c_tiles[:, tiles, :], in_=c_dram[:, tiles, :])
+
+        def load_weights(w, block, name):
+            cols = slice(block * BLOCK, (block + 1) * BLOCK)
+            raw = raw_pool.tile([P, PASSES * PACK, BLOCK], BF16, tag="raw", name=name)
+            rows = w[:, cols].rearrange("(c p t) n -> c p t n", p=P, t=PACK)
+            for c in range(PASSES):
+                nc.sync.dma_start(out=raw[:, c * PACK : (c + 1) * PACK, :], in_=rows[c])
+            return raw
+
+        raws = []
+        raws.append(load_weights(W_lin, 0, "raw_lin0"))
+        load_tokens(0)
+        load_tokens(1)
+        raws.append(load_weights(W_gate, 0, "raw_gate0"))
+        for block in range(1, BLOCKS):
+            raws.append(load_weights(W_lin, block, "raw_lin%d" % block))
+            raws.append(load_weights(W_gate, block, "raw_gate%d" % block))
+
+        grouped = keep.tile([P, PASSES * TOKENS * PACK], BF16, align_bytes=64)
+        grouped_values = grouped[:].rearrange("p (c r t) -> p c r t", c=PASSES, t=PACK)
+        grouped_words = grouped[:].bitcast(F32).rearrange("p (c r u) -> p c r u", c=PASSES, u=2)
+        cat_codes = keep.tile([P, PASSES, TOKENS], U32, align_bytes=64)
+        cat_scales = keep.tile([P, PASSES, TOKENS], U8, align_bytes=64)
+
+        def prepare_tokens(half):
+            first = half * TILES_PER_HALF
+            toks = slice(half * HALF, (half + 1) * HALF)
+            for source in range(2):
+                for i in range(first, first + TILES_PER_HALF, 2):
+                    for g in range(QUERY_PASSES):
+                        c = source * QUERY_PASSES + g
+                        flipped = flip_pool.tile([P, 2, 2, P], F32, tag="flip")
+                        for a in range(2):
+                            for u in range(2):
+                                w0 = (i + a) * (FEATURES // 2) + g * (K_PASS // 2)
+                                nc.tensor.transpose(
+                                    flipped[:, a, u, :], words[source][:, w0 + u : w0 + 2 * P : 2], ident_f32[:]
+                                )
+                        dst = grouped_words[:, c, i * P : (i + 2) * P, :].rearrange("p (a r) u -> p a r u", a=2)
+                        src = flipped[:].rearrange("p a u r -> p a r u")
+                        if g == 0:
+                            nc.scalar.copy(out=dst, in_=src)
+                        else:
+                            nc.vector.tensor_copy(out=dst, in_=src)
+                for g in range(QUERY_PASSES):
+                    c = source * QUERY_PASSES + g
+                    start = (c * TOKENS + half * HALF) * PACK
+                    nc.vector.quantize_mx(
+                        out=cat_codes[:, c, toks].bitcast(FP8X4),
+                        scales=cat_scales[:, c, toks],
+                        in_=grouped[:, start : start + HALF * PACK],
+                    )
+
+        def regroup_weights(raw, scalar_passes):
+            grouped_w = grouped_pool.tile([P, PASSES, SLICES, P, PACK], BF16, align_bytes=64, tag="grouped_w")
+            for c in range(PASSES):
+                for s in range(SLICES):
+                    dst = grouped_w[:, c, s].rearrange("p (a i) t -> p a t i", i=4)
+                    src = raw[:, c * PACK : (c + 1) * PACK, s:BLOCK:SLICES].rearrange("p t (a i) -> p a t i", i=4)
+                    if c < scalar_passes:
+                        nc.scalar.copy(out=dst, in_=src)
+                    else:
+                        nc.vector.tensor_copy(out=dst, in_=src)
+            return grouped_w
+
+        def quantise_weights(grouped_w):
+            codes = weight_pool.tile([P, PASSES, BLOCK], U32, align_bytes=64, tag="codes")
+            scales = weight_pool.tile([P, PASSES, BLOCK], U8, align_bytes=64, tag="scales")
+            for first in range(0, PASSES, 2):
+                nc.vector.quantize_mx(
+                    out=codes[:, first : first + 2, :].rearrange("p c n -> p (c n)").bitcast(FP8X4),
+                    scales=scales[:, first : first + 2, :].rearrange("p c n -> p (c n)"),
+                    in_=grouped_w[:, first : first + 2].rearrange("p c s j t -> p (c s j t)"),
+                )
+            return codes, scales
+
+        def multiply(weights, s, half):
+            codes, scales = weights
+            feats = slice(s * P, (s + 1) * P)
+            toks = slice(half * HALF, (half + 1) * HALF)
+            acc = acc_pool.tile([P, HALF], F32, tag="acc")
+            for c in range(PASSES):
+                nc.tensor.matmul_mx(
+                    out=acc[:],
+                    lhsT=codes[:, c, feats].bitcast(FP8X4),
+                    lhsT_scale=scales[:, c, feats],
+                    rhs=cat_codes[:, c, toks].bitcast(FP8X4),
+                    rhs_scale=cat_scales[:, c, toks],
+                    start=(c == 0),
+                    stop=(c == PASSES - 1),
+                )
+            return acc
+
+        mixes = {}
+        aways = {}
+        backs = {}
+
+        def step(m, weights):
+            block = m // 2
+            for half in range(HALVES):
+                if m % 2 == 0:
+                    value = hidden_pool.tile([P, SLICES, HALF], F32, tag="mix")
+                    mixes[(block, half)] = value
+                else:
+                    value = gate_pool.tile([P, SLICES, HALF], F32, tag="away")
+                    aways[(block, half)] = value
+                for s in range(SLICES):
+                    n = block * SLICES + s
+                    acc = multiply(weights, s, half)
+                    if m % 2 == 0:
+                        nc.scalar.activation(
+                            out=value[:, s, :], in_=acc[:], func=ACT.Tanh, bias=bias_lin[:, n : n + 1], scale=1.0
+                        )
+                    else:
+                        nc.scalar.activation(
+                            out=value[:, s, :], in_=acc[:], func=ACT.Sigmoid, bias=neg_bias_gate[:, n : n + 1], scale=-1.0
+                        )
+
+        def subtract_query(block):
+            for half in range(HALVES):
+                mix = mixes[(block, half)]
+                toks = slice(half * HALF, (half + 1) * HALF)
+                q_t = grouped_values[:, block, toks, :].rearrange("p r s -> p s r")
+                nc.vector.tensor_sub(out=mix[:], in0=mix[:], in1=q_t)
+
+        def weigh(block):
+            for half in range(HALVES):
+                mix = mixes[(block, half)]
+                nc.vector.tensor_mul(out=mix[:], in0=mix[:], in1=aways[(block, half)][:])
+
+        def transpose_back(block):
+            for half in range(HALVES):
+                for i in range(TILES_PER_HALF):
+                    back = flip_pool.tile([P, SLICES, P], F32, tag="flip")
+                    for s in range(SLICES):
+                        nc.tensor.transpose(
+                            back[:, s, :], mixes[(block, half)][:, s, i * P : (i + 1) * P], ident_f32[:]
+                        )
+                    backs[(block, half, i)] = back
+
+        def add_query_and_store(block):
+            cols = slice(block * BLOCK, (block + 1) * BLOCK)
+            for half in range(HALVES):
+                for i in range(TILES_PER_HALF):
+                    tile_index = half * TILES_PER_HALF + i
+                    result = result_pool.tile([P, BLOCK], F32, tag="result")
+                    nc.vector.tensor_add(
+                        out=result[:].rearrange("p (j s) -> p j s", s=SLICES),
+                        in0=backs[(block, half, i)][:].rearrange("p s j -> p j s"),
+                        in1=q_tiles[:, tile_index, cols].rearrange("p (j s) -> p j s", s=SLICES),
+                    )
+                    nc.sync.dma_start(out=out_dram[:, tile_index, cols], in_=result[:])
+
+        def scalar_share(m):
+            return 2 if m < EARLY_STEPS else 3
+
+        weights = quantise_weights(regroup_weights(raws[0], scalar_share(0)))
+        prepare_tokens(0)
+
+        bias_cols = flip_pool.tile([P, 2, P], F32, tag="flip")
+        for u in range(2):
+            nc.tensor.transpose(bias_cols[:, u, :], bias_rows[:].bitcast(F32)[:, u : 2 * P : 2], ident_f32[:])
+        bias_values = bias_cols[:].rearrange("p u r -> p (u r)").bitcast(BF16).rearrange("p (u r e) -> p r u e", u=2, e=2)
+        bias_lin = keep.tile([P, 8], F32)
+        nc.vector.tensor_copy(out=bias_lin[:].rearrange("p (r u e) -> p r u e", r=2, u=2), in_=bias_values[:, 0:2])
+        neg_bias_gate = keep.tile([P, 8], F32)
+        nc.vector.tensor_scalar_mul(
+            out=neg_bias_gate[:].rearrange("p (r u e) -> p r u e", r=2, u=2), in0=bias_values[:, 2:4], scalar1=-1.0
+        )
+
+        prepare_tokens(1)
+
+        for m in range(STEPS + 2):
+            if m + 1 < STEPS:
+                grouped_next = regroup_weights(raws[m + 1], scalar_share(m + 1))
+            if m < STEPS:
+                step(m, weights)
+            if m % 2 == 1 and m >= 3:
+                add_query_and_store((m - 3) // 2)
+            if m % 2 == 0 and m >= 2:
+                weigh((m - 2) // 2)
+                transpose_back((m - 2) // 2)
+            if m + 1 < STEPS:
+                weights = quantise_weights(grouped_next)
+            if m % 2 == 1 and m < STEPS:
+                subtract_query((m - 1) // 2)

@@ -22,11 +22,13 @@ TOKEN_TILES = TOKENS // P
 HALF = 512
 HALVES = TOKENS // HALF
 TILES_PER_HALF = HALF // P
+HALF_TOKENS = [slice(h * HALF, (h + 1) * HALF) for h in range(HALVES)]
+ALL_TOKENS = slice(0, TOKENS)
 BLOCK = 512
 BLOCKS = FEATURES // BLOCK
 SLICES = BLOCK // P
 STEPS = 2 * BLOCKS
-EARLY_STEPS = 2
+CHUNK = 4
 
 FLOPS = 2 * TOKENS * 2 * FEATURES * 2 * FEATURES
 
@@ -36,17 +38,55 @@ def tile_smcmr_pb_kernel(tc, query, weighted_ctx, W_lin, b_lin, W_gate, b_gate, 
     q_dram = query.flatten_outer_dims().rearrange("(p i) d -> p i d", i=TOKEN_TILES)
     c_dram = weighted_ctx.flatten_outer_dims().rearrange("(p i) d -> p i d", i=TOKEN_TILES)
     out_dram = out.flatten_outer_dims().rearrange("(p i) d -> p i d", i=TOKEN_TILES)
+    w_dram = [w.rearrange("(c p t) n -> c p t n", p=P, t=PACK) for w in (W_lin, W_gate)]
 
     with ExitStack() as ctx:
         keep = ctx.enter_context(tc.tile_pool(name="keep", bufs=1))
         raw_pool = ctx.enter_context(tc.tile_pool(name="raw", bufs=3))
-        grouped_pool = ctx.enter_context(tc.tile_pool(name="grouped", bufs=2))
-        weight_pool = ctx.enter_context(tc.tile_pool(name="weights", bufs=2))
-        hidden_pool = ctx.enter_context(tc.tile_pool(name="hidden", bufs=3))
-        gate_pool = ctx.enter_context(tc.tile_pool(name="gate", bufs=2))
+        grouped_pool = ctx.enter_context(tc.tile_pool(name="grouped", bufs=4))
+        weight_pool = ctx.enter_context(tc.tile_pool(name="weights", bufs=8))
+        hidden_pool = ctx.enter_context(tc.tile_pool(name="hidden", bufs=2))
+        gate_pool = ctx.enter_context(tc.tile_pool(name="gate", bufs=1))
         result_pool = ctx.enter_context(tc.tile_pool(name="result", bufs=4))
         acc_pool = ctx.enter_context(tc.psum_pool(name="acc", bufs=4))
         flip_pool = ctx.enter_context(tc.psum_pool(name="flip", bufs=4))
+        ctx.enter_context(tc.manual_schedule())
+
+        q_sb = keep.tile([P, TOKEN_TILES * FEATURES], BF16)
+        q_tiles = q_sb[:].rearrange("p (i d) -> p i d", i=TOKEN_TILES)
+        c_sb = keep.tile([P, TOKEN_TILES * FEATURES], BF16)
+        c_tiles = c_sb[:].rearrange("p (i d) -> p i d", i=TOKEN_TILES)
+        words = [q_sb[:].bitcast(F32), c_sb[:].bitcast(F32)]
+        bias_lin_raw = keep.tile([P, BLOCKS, SLICES], BF16)
+        bias_gate_raw = keep.tile([P, BLOCKS, SLICES], BF16)
+        nc.scalar.dma_start(out=bias_lin_raw[:], in_=b_lin.rearrange("(b j s) -> j b s", j=P, s=SLICES))
+        nc.scalar.dma_start(out=bias_gate_raw[:], in_=b_gate.rearrange("(b j s) -> j b s", j=P, s=SLICES))
+        raws = []
+
+        def load_tokens(source, first):
+            tiles, dram = ((q_tiles, q_dram), (c_tiles, c_dram))[source]
+            nc.sync.dma_start(out=tiles[:, first : first + 2, :], in_=dram[:, first : first + 2, :])
+
+        def load_weights(m, c):
+            if len(raws) == m:
+                raw = raw_pool.tile([P, PASSES, PACK, BLOCK], BF16, tag="raw", name="raw%d" % m)
+                raws.append(raw)
+            cols = slice((m // 2) * BLOCK, (m // 2 + 1) * BLOCK)
+            nc.sync.dma_start(out=raws[m][:, c], in_=w_dram[m % 2][c, :, :, cols])
+
+        load_tokens(0, 0)
+        load_tokens(0, 2)
+        load_weights(0, 0)
+        load_tokens(1, 0)
+        load_tokens(1, 2)
+        for c in range(1, PASSES):
+            load_weights(0, c)
+        for source in range(2):
+            load_tokens(source, 4)
+            load_tokens(source, 6)
+        for m in range(1, STEPS):
+            for c in range(PASSES):
+                load_weights(m, c)
 
         ident_f32 = keep.tile([P, P], F32)
         masks.make_identity(nc, ident_f32[:])
@@ -56,38 +96,17 @@ def tile_smcmr_pb_kernel(tc, query, weighted_ctx, W_lin, b_lin, W_gate, b_gate, 
         nc.vector.memset(warm_in[:], 0.0)
         nc.scalar.activation(out=warm_out[:], in_=warm_in[:], func=ACT.Sigmoid)
 
-        bias_rows = keep.tile([P, BLOCK], BF16)
-        nc.vector.memset(bias_rows[:], 0.0)
-        nc.scalar.dma_start(out=bias_rows[0:BLOCKS, :], in_=b_lin.rearrange("(b n) -> b n", n=BLOCK))
-        nc.scalar.dma_start(out=bias_rows[BLOCKS : 2 * BLOCKS, :], in_=b_gate.rearrange("(b n) -> b n", n=BLOCK))
-
-        q_sb = keep.tile([P, TOKEN_TILES * FEATURES], BF16)
-        q_tiles = q_sb[:].rearrange("p (i d) -> p i d", i=TOKEN_TILES)
-        c_sb = keep.tile([P, TOKEN_TILES * FEATURES], BF16)
-        c_tiles = c_sb[:].rearrange("p (i d) -> p i d", i=TOKEN_TILES)
-        words = [q_sb[:].bitcast(F32), c_sb[:].bitcast(F32)]
-
-        def load_tokens(half):
-            tiles = slice(half * TILES_PER_HALF, (half + 1) * TILES_PER_HALF)
-            nc.sync.dma_start(out=q_tiles[:, tiles, :], in_=q_dram[:, tiles, :])
-            nc.sync.dma_start(out=c_tiles[:, tiles, :], in_=c_dram[:, tiles, :])
-
-        def load_weights(w, block, name):
-            cols = slice(block * BLOCK, (block + 1) * BLOCK)
-            raw = raw_pool.tile([P, PASSES * PACK, BLOCK], BF16, tag="raw", name=name)
-            rows = w[:, cols].rearrange("(c p t) n -> c p t n", p=P, t=PACK)
-            for c in range(PASSES):
-                nc.sync.dma_start(out=raw[:, c * PACK : (c + 1) * PACK, :], in_=rows[c])
-            return raw
-
-        raws = []
-        raws.append(load_weights(W_lin, 0, "raw_lin0"))
-        load_tokens(0)
-        load_tokens(1)
-        raws.append(load_weights(W_gate, 0, "raw_gate0"))
-        for block in range(1, BLOCKS):
-            raws.append(load_weights(W_lin, block, "raw_lin%d" % block))
-            raws.append(load_weights(W_gate, block, "raw_gate%d" % block))
+        bias_lin = keep.tile([P, BLOCKS * SLICES], F32)
+        neg_bias_gate = keep.tile([P, BLOCKS * SLICES], F32)
+        nc.gpsimd.tensor_copy(out=bias_lin[:], in_=bias_lin_raw[:].rearrange("p b s -> p (b s)"))
+        nc.gpsimd.tensor_scalar(
+            out=neg_bias_gate[:],
+            in0=bias_gate_raw[:].rearrange("p b s -> p (b s)"),
+            scalar1=-1.0,
+            scalar2=0.0,
+            op0=ALU.mult,
+            op1=ALU.add,
+        )
 
         grouped = keep.tile([P, PASSES * TOKENS * PACK], BF16, align_bytes=64)
         grouped_values = grouped[:].rearrange("p (c r t) -> p c r t", c=PASSES, t=PACK)
@@ -95,165 +114,240 @@ def tile_smcmr_pb_kernel(tc, query, weighted_ctx, W_lin, b_lin, W_gate, b_gate, 
         cat_codes = keep.tile([P, PASSES, TOKENS], U32, align_bytes=64)
         cat_scales = keep.tile([P, PASSES, TOKENS], U8, align_bytes=64)
 
-        def prepare_tokens(half):
-            first = half * TILES_PER_HALF
+        def flip_tokens(source, first, engines):
+            for g in range(QUERY_PASSES):
+                c = source * QUERY_PASSES + g
+                flipped = flip_pool.tile([P, 2, 2, P], F32, tag="flip")
+                for a in range(2):
+                    for u in range(2):
+                        w0 = (first + a) * (FEATURES // 2) + g * (K_PASS // 2)
+                        nc.tensor.transpose(
+                            flipped[:, a, u, :], words[source][:, w0 + u : w0 + 2 * P : 2], ident_f32[:]
+                        )
+                dst = grouped_words[:, c, first * P : (first + 2) * P, :].rearrange("p (a r) u -> p a r u", a=2)
+                src = flipped[:].rearrange("p a u r -> p a r u")
+                if engines[g] == "scalar":
+                    nc.scalar.copy(out=dst, in_=src)
+                else:
+                    nc.vector.tensor_copy(out=dst, in_=src)
+
+        def quantise_tokens(source, half):
             toks = slice(half * HALF, (half + 1) * HALF)
-            for source in range(2):
-                for i in range(first, first + TILES_PER_HALF, 2):
-                    for g in range(QUERY_PASSES):
-                        c = source * QUERY_PASSES + g
-                        flipped = flip_pool.tile([P, 2, 2, P], F32, tag="flip")
-                        for a in range(2):
-                            for u in range(2):
-                                w0 = (i + a) * (FEATURES // 2) + g * (K_PASS // 2)
-                                nc.tensor.transpose(
-                                    flipped[:, a, u, :], words[source][:, w0 + u : w0 + 2 * P : 2], ident_f32[:]
-                                )
-                        dst = grouped_words[:, c, i * P : (i + 2) * P, :].rearrange("p (a r) u -> p a r u", a=2)
-                        src = flipped[:].rearrange("p a u r -> p a r u")
-                        if g == 0:
-                            nc.scalar.copy(out=dst, in_=src)
-                        else:
-                            nc.vector.tensor_copy(out=dst, in_=src)
-                for g in range(QUERY_PASSES):
-                    c = source * QUERY_PASSES + g
-                    start = (c * TOKENS + half * HALF) * PACK
-                    nc.vector.quantize_mx(
-                        out=cat_codes[:, c, toks].bitcast(FP8X4),
-                        scales=cat_scales[:, c, toks],
-                        in_=grouped[:, start : start + HALF * PACK],
-                    )
-
-        def regroup_weights(raw, scalar_passes):
-            grouped_w = grouped_pool.tile([P, PASSES, SLICES, P, PACK], BF16, align_bytes=64, tag="grouped_w")
-            for c in range(PASSES):
-                for s in range(SLICES):
-                    dst = grouped_w[:, c, s].rearrange("p (a i) t -> p a t i", i=4)
-                    src = raw[:, c * PACK : (c + 1) * PACK, s:BLOCK:SLICES].rearrange("p t (a i) -> p a t i", i=4)
-                    if c < scalar_passes:
-                        nc.scalar.copy(out=dst, in_=src)
-                    else:
-                        nc.vector.tensor_copy(out=dst, in_=src)
-            return grouped_w
-
-        def quantise_weights(grouped_w):
-            codes = weight_pool.tile([P, PASSES, BLOCK], U32, align_bytes=64, tag="codes")
-            scales = weight_pool.tile([P, PASSES, BLOCK], U8, align_bytes=64, tag="scales")
-            for first in range(0, PASSES, 2):
+            for g in range(QUERY_PASSES):
+                c = source * QUERY_PASSES + g
+                start = (c * TOKENS + half * HALF) * PACK
                 nc.vector.quantize_mx(
-                    out=codes[:, first : first + 2, :].rearrange("p c n -> p (c n)").bitcast(FP8X4),
-                    scales=scales[:, first : first + 2, :].rearrange("p c n -> p (c n)"),
-                    in_=grouped_w[:, first : first + 2].rearrange("p c s j t -> p (c s j t)"),
+                    out=cat_codes[:, c, toks].bitcast(FP8X4),
+                    scales=cat_scales[:, c, toks],
+                    in_=grouped[:, start : start + HALF * PACK],
                 )
-            return codes, scales
 
-        def multiply(weights, s, half):
-            codes, scales = weights
-            feats = slice(s * P, (s + 1) * P)
-            toks = slice(half * HALF, (half + 1) * HALF)
-            acc = acc_pool.tile([P, HALF], F32, tag="acc")
-            for c in range(PASSES):
+        grouped_w = {}
+        weights = {}
+
+        def regroup(m, chunk, first, engine):
+            if (m, chunk) not in grouped_w:
+                tile = grouped_pool.tile([P, CHUNK, P, PACK], BF16, align_bytes=64, tag="grouped_w")
+                grouped_w[(m, chunk)] = tile
+            dst = grouped_w[(m, chunk)][:, first : first + 2].rearrange("p x (a i) t -> p x a t i", i=4)
+            values = raws[m][:].rearrange("p c t (j s) -> p c s t j", s=SLICES)
+            if m == 0:
+                src = values[:, chunk, first : first + 2]
+            else:
+                src = values[:, first : first + 2, chunk]
+            src = src.rearrange("p x t (a i) -> p x a t i", i=4)
+            if engine == "scalar":
+                nc.scalar.copy(out=dst, in_=src)
+            else:
+                nc.vector.tensor_copy(out=dst, in_=src)
+
+        def quantise(m, chunk):
+            codes = weight_pool.tile([P, CHUNK, P], U32, align_bytes=64, tag="codes")
+            scales = weight_pool.tile([P, CHUNK, P], U8, align_bytes=64, tag="scales")
+            weights[(m, chunk)] = (codes, scales)
+            nc.vector.quantize_mx(
+                out=codes[:].rearrange("p x n -> p (x n)").bitcast(FP8X4),
+                scales=scales[:].rearrange("p x n -> p (x n)"),
+                in_=grouped_w[(m, chunk)][:].rearrange("p x j t -> p (x j t)"),
+            )
+
+        def multiply(acc, m, s, toks, passes):
+            for c in passes:
+                chunk, x = (c, s) if m == 0 else (s, c)
+                codes, scales = weights[(m, chunk)]
                 nc.tensor.matmul_mx(
                     out=acc[:],
-                    lhsT=codes[:, c, feats].bitcast(FP8X4),
-                    lhsT_scale=scales[:, c, feats],
+                    lhsT=codes[:, x, :].bitcast(FP8X4),
+                    lhsT_scale=scales[:, x, :],
                     rhs=cat_codes[:, c, toks].bitcast(FP8X4),
                     rhs_scale=cat_scales[:, c, toks],
                     start=(c == 0),
                     stop=(c == PASSES - 1),
                 )
-            return acc
 
         mixes = {}
         aways = {}
         backs = {}
 
-        def step(m, weights):
+        def activate(acc, m, s, toks):
             block = m // 2
-            for half in range(HALVES):
-                if m % 2 == 0:
-                    value = hidden_pool.tile([P, SLICES, HALF], F32, tag="mix")
-                    mixes[(block, half)] = value
-                else:
-                    value = gate_pool.tile([P, SLICES, HALF], F32, tag="away")
-                    aways[(block, half)] = value
-                for s in range(SLICES):
-                    n = block * SLICES + s
-                    acc = multiply(weights, s, half)
-                    if m % 2 == 0:
-                        nc.scalar.activation(
-                            out=value[:, s, :], in_=acc[:], func=ACT.Tanh, bias=bias_lin[:, n : n + 1], scale=1.0
-                        )
-                    else:
-                        nc.scalar.activation(
-                            out=value[:, s, :], in_=acc[:], func=ACT.Sigmoid, bias=neg_bias_gate[:, n : n + 1], scale=-1.0
-                        )
+            n = block * SLICES + s
+            if m % 2 == 0:
+                if block not in mixes:
+                    mix = hidden_pool.tile([P, SLICES, TOKENS], F32, tag="mix")
+                    mixes[block] = mix
+                nc.scalar.activation(
+                    out=mixes[block][:, s, toks], in_=acc[:], func=ACT.Tanh, bias=bias_lin[:, n : n + 1], scale=1.0
+                )
+            else:
+                if block not in aways:
+                    away = gate_pool.tile([P, SLICES, TOKENS], F32, tag="away")
+                    aways[block] = away
+                nc.scalar.activation(
+                    out=aways[block][:, s, toks],
+                    in_=acc[:],
+                    func=ACT.Sigmoid,
+                    bias=neg_bias_gate[:, n : n + 1],
+                    scale=-1.0,
+                )
 
-        def subtract_query(block):
-            for half in range(HALVES):
-                mix = mixes[(block, half)]
-                toks = slice(half * HALF, (half + 1) * HALF)
-                q_t = grouped_values[:, block, toks, :].rearrange("p r s -> p s r")
-                nc.vector.tensor_sub(out=mix[:], in0=mix[:], in1=q_t)
+        def subtract_query(block, s, toks):
+            mix = mixes[block][:, s, toks]
+            nc.vector.tensor_sub(out=mix, in0=mix, in1=grouped_values[:, block, toks, s])
 
-        def weigh(block):
-            for half in range(HALVES):
-                mix = mixes[(block, half)]
-                nc.vector.tensor_mul(out=mix[:], in0=mix[:], in1=aways[(block, half)][:])
+        def weigh(block, s, toks):
+            mix = mixes[block][:, s, toks]
+            nc.vector.tensor_mul(out=mix, in0=mix, in1=aways[block][:, s, toks])
 
-        def transpose_back(block):
-            for half in range(HALVES):
-                for i in range(TILES_PER_HALF):
-                    back = flip_pool.tile([P, SLICES, P], F32, tag="flip")
-                    for s in range(SLICES):
-                        nc.tensor.transpose(
-                            back[:, s, :], mixes[(block, half)][:, s, i * P : (i + 1) * P], ident_f32[:]
-                        )
-                    backs[(block, half, i)] = back
-
-        def add_query_and_store(block):
-            cols = slice(block * BLOCK, (block + 1) * BLOCK)
-            for half in range(HALVES):
-                for i in range(TILES_PER_HALF):
-                    tile_index = half * TILES_PER_HALF + i
-                    result = result_pool.tile([P, BLOCK], F32, tag="result")
-                    nc.vector.tensor_add(
-                        out=result[:].rearrange("p (j s) -> p j s", s=SLICES),
-                        in0=backs[(block, half, i)][:].rearrange("p s j -> p j s"),
-                        in1=q_tiles[:, tile_index, cols].rearrange("p (j s) -> p j s", s=SLICES),
+        def transpose_back(block, tiles, slices, pool, tag):
+            for i in tiles:
+                if (block, i) not in backs:
+                    back = pool.tile([P, SLICES, P], F32, tag=tag, name="back")
+                    backs[(block, i)] = back
+                for s in slices:
+                    nc.tensor.transpose(
+                        backs[(block, i)][:, s, :], mixes[block][:, s, i * P : (i + 1) * P], ident_f32[:]
                     )
-                    nc.sync.dma_start(out=out_dram[:, tile_index, cols], in_=result[:])
 
-        def scalar_share(m):
-            return 2 if m < EARLY_STEPS else 3
+        def add_query_and_store(block, tiles):
+            cols = slice(block * BLOCK, (block + 1) * BLOCK)
+            for i in tiles:
+                result = result_pool.tile([P, BLOCK], F32, tag="result")
+                nc.vector.tensor_add(
+                    out=result[:].rearrange("p (j s) -> p j s", s=SLICES),
+                    in0=backs[(block, i)][:].rearrange("p s j -> p j s"),
+                    in1=q_tiles[:, i, cols].rearrange("p (j s) -> p j s", s=SLICES),
+                )
+                nc.sync.dma_start(out=out_dram[:, i, cols], in_=result[:])
 
-        weights = quantise_weights(regroup_weights(raws[0], scalar_share(0)))
-        prepare_tokens(0)
+        accs = []
 
-        bias_cols = flip_pool.tile([P, 2, P], F32, tag="flip")
-        for u in range(2):
-            nc.tensor.transpose(bias_cols[:, u, :], bias_rows[:].bitcast(F32)[:, u : 2 * P : 2], ident_f32[:])
-        bias_values = bias_cols[:].rearrange("p u r -> p (u r)").bitcast(BF16).rearrange("p (u r e) -> p r u e", u=2, e=2)
-        bias_lin = keep.tile([P, 8], F32)
-        nc.vector.tensor_copy(out=bias_lin[:].rearrange("p (r u e) -> p r u e", r=2, u=2), in_=bias_values[:, 0:2])
-        neg_bias_gate = keep.tile([P, 8], F32)
-        nc.vector.tensor_scalar_mul(
-            out=neg_bias_gate[:].rearrange("p (r u e) -> p r u e", r=2, u=2), in0=bias_values[:, 2:4], scalar1=-1.0
-        )
+        def head_pass(c):
+            for s in range(SLICES):
+                if c == 0:
+                    acc = acc_pool.tile([P, HALF], F32, tag="acc", name="acc")
+                    accs.append(acc)
+                multiply(accs[s], 0, s, HALF_TOKENS[0], (c,))
 
-        prepare_tokens(1)
+        S, V = "scalar", "vector"
+        flip_tokens(0, 0, (S, V))
+        flip_tokens(0, 2, (S, V))
+        regroup(0, 0, 0, S)
+        regroup(0, 0, 2, V)
+        quantise_tokens(0, 0)
+        quantise(0, 0)
+        flip_tokens(1, 0, (S, S))
+        flip_tokens(1, 2, (S, S))
+        head_pass(0)
+        regroup(0, 1, 0, S)
+        regroup(0, 1, 2, V)
+        quantise_tokens(1, 0)
+        quantise(0, 1)
+        regroup(0, 2, 0, S)
+        regroup(0, 2, 2, V)
+        regroup(0, 3, 0, S)
+        regroup(0, 3, 2, V)
+        quantise(0, 2)
+        quantise(0, 3)
+        flip_tokens(0, 4, (S, V))
+        head_pass(1)
+        flip_tokens(0, 6, (S, V))
+        quantise_tokens(0, 1)
+        head_pass(2)
+        flip_tokens(1, 4, (S, V))
+        flip_tokens(1, 6, (S, V))
+        head_pass(3)
+        quantise_tokens(1, 1)
+        for s in range(SLICES):
+            activate(accs[s], 0, s, HALF_TOKENS[0])
 
-        for m in range(STEPS + 2):
-            if m + 1 < STEPS:
-                grouped_next = regroup_weights(raws[m + 1], scalar_share(m + 1))
-            if m < STEPS:
-                step(m, weights)
-            if m % 2 == 1 and m >= 3:
-                add_query_and_store((m - 3) // 2)
-            if m % 2 == 0 and m >= 2:
-                weigh((m - 2) // 2)
-                transpose_back((m - 2) // 2)
-            if m + 1 < STEPS:
-                weights = quantise_weights(grouped_next)
-            if m % 2 == 1 and m < STEPS:
-                subtract_query((m - 1) // 2)
+        def group(m, s, toks):
+            acc = acc_pool.tile([P, toks.stop - toks.start], F32, tag="acc", name="acc")
+            multiply(acc, m, s, toks, range(PASSES))
+            activate(acc, m, s, toks)
+
+        slots = [(0, s, HALF_TOKENS[1]) for s in range(SLICES)]
+        for m in (1, 2):
+            slots += [(m, s, toks) for s in range(SLICES) for toks in HALF_TOKENS]
+        chunks = [(m, s) for m in (1, 2, 3) for s in range(SLICES)]
+        half_0, half_1 = HALF_TOKENS
+
+        def prepare(i):
+            if i < len(chunks):
+                regroup(*chunks[i], 0, S)
+                regroup(*chunks[i], 2, S if i in (4, 8) else V)
+
+        for j in range(len(slots) // 2):
+            prepare(j)
+            if j == 9:
+                prepare(10)
+            if 1 <= j:
+                quantise(*chunks[j - 1])
+            group(*slots[2 * j])
+            if j == 0:
+                for s in range(SLICES):
+                    subtract_query(0, s, half_0)
+            if j == 1 or j == 2:
+                for s in (2 * j - 2, 2 * j - 1):
+                    subtract_query(0, s, half_1)
+            group(*slots[2 * j + 1])
+            if 3 <= j <= 6:
+                weigh(0, j - 3, ALL_TOKENS)
+            if j == 6:
+                transpose_back(0, range(0, 4), range(SLICES), flip_pool, "flip")
+            if j == 7:
+                add_query_and_store(0, range(0, 4))
+                transpose_back(0, range(4, 8), range(SLICES), flip_pool, "flip")
+            if j == 8:
+                add_query_and_store(0, range(4, 6))
+            if j == 9:
+                add_query_and_store(0, range(6, 8))
+                subtract_query(1, 0, ALL_TOKENS)
+        quantise(3, 1)
+        prepare(11)
+        group(3, 0, half_0)
+        quantise(3, 2)
+        group(3, 1, half_0)
+        subtract_query(1, 1, ALL_TOKENS)
+        quantise(3, 3)
+        group(3, 2, half_0)
+        weigh(1, 0, half_0)
+        weigh(1, 1, half_0)
+        group(3, 3, half_0)
+        subtract_query(1, 2, ALL_TOKENS)
+        weigh(1, 2, half_0)
+        subtract_query(1, 3, ALL_TOKENS)
+        weigh(1, 3, half_0)
+        quarters = (slice(512, 768), slice(768, 1024))
+        for part, toks in enumerate(quarters):
+            for s in range(SLICES):
+                group(3, s, toks)
+                if part == 0 and s == 1:
+                    transpose_back(1, range(0, 4), range(SLICES), flip_pool, "flip")
+                    add_query_and_store(1, range(0, 4))
+                if part == 1 and s == 1:
+                    transpose_back(1, range(4, 6), range(SLICES), flip_pool, "flip")
+                    add_query_and_store(1, range(4, 6))
+                weigh(1, s, toks)
+        transpose_back(1, range(6, 8), range(SLICES), flip_pool, "flip")
+        add_query_and_store(1, range(6, 8))

@@ -50,7 +50,6 @@ def tile_smcmr_pb_kernel(tc, query, weighted_ctx, W_lin, b_lin, W_gate, b_gate, 
         result_pool = ctx.enter_context(tc.tile_pool(name="result", bufs=4))
         acc_pool = ctx.enter_context(tc.psum_pool(name="acc", bufs=4))
         flip_pool = ctx.enter_context(tc.psum_pool(name="flip", bufs=4))
-        ctx.enter_context(tc.manual_schedule())
 
         q_sb = keep.tile([P, TOKEN_TILES * FEATURES], BF16)
         q_tiles = q_sb[:].rearrange("p (i d) -> p i d", i=TOKEN_TILES)
@@ -59,8 +58,6 @@ def tile_smcmr_pb_kernel(tc, query, weighted_ctx, W_lin, b_lin, W_gate, b_gate, 
         words = [q_sb[:].bitcast(F32), c_sb[:].bitcast(F32)]
         bias_lin_raw = keep.tile([P, BLOCKS, SLICES], BF16)
         bias_gate_raw = keep.tile([P, BLOCKS, SLICES], BF16)
-        nc.scalar.dma_start(out=bias_lin_raw[:], in_=b_lin.rearrange("(b j s) -> j b s", j=P, s=SLICES))
-        nc.scalar.dma_start(out=bias_gate_raw[:], in_=b_gate.rearrange("(b j s) -> j b s", j=P, s=SLICES))
         raws = []
 
         def load_tokens(source, first):
@@ -84,6 +81,8 @@ def tile_smcmr_pb_kernel(tc, query, weighted_ctx, W_lin, b_lin, W_gate, b_gate, 
         for source in range(2):
             load_tokens(source, 4)
             load_tokens(source, 6)
+        nc.sync.dma_start(out=bias_lin_raw[:], in_=b_lin.rearrange("(b j s) -> j b s", j=P, s=SLICES))
+        nc.sync.dma_start(out=bias_gate_raw[:], in_=b_gate.rearrange("(b j s) -> j b s", j=P, s=SLICES))
         for m in range(1, STEPS):
             for c in range(PASSES):
                 load_weights(m, c)
@@ -270,12 +269,12 @@ def tile_smcmr_pb_kernel(tc, query, weighted_ctx, W_lin, b_lin, W_gate, b_gate, 
         quantise(0, 2)
         quantise(0, 3)
         flip_tokens(0, 4, (S, V))
-        head_pass(1)
         flip_tokens(0, 6, (S, V))
         quantise_tokens(0, 1)
-        head_pass(2)
         flip_tokens(1, 4, (S, V))
         flip_tokens(1, 6, (S, V))
+        head_pass(1)
+        head_pass(2)
         head_pass(3)
         quantise_tokens(1, 1)
         for s in range(SLICES):
@@ -295,7 +294,7 @@ def tile_smcmr_pb_kernel(tc, query, weighted_ctx, W_lin, b_lin, W_gate, b_gate, 
         def prepare(i):
             if i < len(chunks):
                 regroup(*chunks[i], 0, S)
-                regroup(*chunks[i], 2, S if i in (4, 8) else V)
+                regroup(*chunks[i], 2, S if i in (5, 8) else V)
 
         for j in range(len(slots) // 2):
             prepare(j)

@@ -71,16 +71,15 @@ def tile_smcmr_pb_kernel(tc, query, weighted_ctx, W_lin, b_lin, W_gate, b_gate, 
             cols = slice((m // 2) * BLOCK, (m // 2 + 1) * BLOCK)
             nc.sync.dma_start(out=raws[m][:, c], in_=w_dram[m % 2][c, :, :, cols])
 
-        load_tokens(0, 0)
-        load_tokens(0, 2)
-        load_weights(0, 0)
+        for first in range(0, TOKEN_TILES, 2):
+            load_tokens(0, first)
         load_tokens(1, 0)
         load_tokens(1, 2)
+        load_weights(0, 0)
+        load_tokens(1, 4)
+        load_tokens(1, 6)
         for c in range(1, PASSES):
             load_weights(0, c)
-        for source in range(2):
-            load_tokens(source, 4)
-            load_tokens(source, 6)
         nc.sync.dma_start(out=bias_lin_raw[:], in_=b_lin.rearrange("(b j s) -> j b s", j=P, s=SLICES))
         nc.sync.dma_start(out=bias_gate_raw[:], in_=b_gate.rearrange("(b j s) -> j b s", j=P, s=SLICES))
         for m in range(1, STEPS):
@@ -239,103 +238,92 @@ def tile_smcmr_pb_kernel(tc, query, weighted_ctx, W_lin, b_lin, W_gate, b_gate, 
                 )
                 nc.sync.dma_start(out=out_dram[:, i, cols], in_=result[:])
 
-        accs = []
-
-        def head_pass(c):
-            for s in range(SLICES):
-                if c == 0:
-                    acc = acc_pool.tile([P, HALF], F32, tag="acc", name="acc")
-                    accs.append(acc)
-                multiply(accs[s], 0, s, HALF_TOKENS[0], (c,))
-
         S, V = "scalar", "vector"
-        flip_tokens(0, 0, (S, V))
-        flip_tokens(0, 2, (S, V))
-        regroup(0, 0, 0, S)
-        regroup(0, 0, 2, V)
-        quantise_tokens(0, 0)
-        quantise(0, 0)
-        flip_tokens(1, 0, (S, S))
-        flip_tokens(1, 2, (S, S))
-        head_pass(0)
-        regroup(0, 1, 0, S)
-        regroup(0, 1, 2, V)
-        quantise_tokens(1, 0)
-        quantise(0, 1)
-        regroup(0, 2, 0, S)
-        regroup(0, 2, 2, V)
-        regroup(0, 3, 0, S)
-        regroup(0, 3, 2, V)
-        quantise(0, 2)
-        quantise(0, 3)
-        flip_tokens(0, 4, (S, V))
-        flip_tokens(0, 6, (S, V))
-        quantise_tokens(0, 1)
-        flip_tokens(1, 4, (S, V))
-        flip_tokens(1, 6, (S, V))
-        head_pass(1)
-        head_pass(2)
-        head_pass(3)
-        quantise_tokens(1, 1)
-        for s in range(SLICES):
-            activate(accs[s], 0, s, HALF_TOKENS[0])
+        with tc.manual_schedule():
+            for first, engines in ((0, (S, V)), (2, (S, V)), (4, (S, V))):
+                flip_tokens(0, first, engines)
+            quantise_tokens(0, 0)
+            flip_tokens(0, 6, (S, V))
+            quantise_tokens(0, 1)
+            flip_tokens(1, 0, (S, S))
+            flip_tokens(1, 2, (S, S))
+            regroup(0, 0, 0, S)
+            regroup(0, 0, 2, V)
+            quantise_tokens(1, 0)
+            quantise(0, 0)
+            flip_tokens(1, 4, (S, V))
+            flip_tokens(1, 6, (S, V))
+            quantise_tokens(1, 1)
+            for c in range(1, PASSES):
+                regroup(0, c, 0, S)
+                regroup(0, c, 2, V)
+                quantise(0, c)
+            accs = {}
+            for half, (pool, tag) in enumerate(((acc_pool, "acc"), (flip_pool, "flip"))):
+                for s in range(SLICES):
+                    acc = pool.tile([P, HALF], F32, tag=tag, name="acc")
+                    accs[(half, s)] = acc
+            for c in range(PASSES):
+                for half in range(HALVES):
+                    for s in range(SLICES):
+                        multiply(accs[(half, s)], 0, s, HALF_TOKENS[half], (c,))
+            for half in range(HALVES):
+                for s in range(SLICES):
+                    activate(accs[(half, s)], 0, s, HALF_TOKENS[half])
 
         def group(m, s, toks):
             acc = acc_pool.tile([P, toks.stop - toks.start], F32, tag="acc", name="acc")
             multiply(acc, m, s, toks, range(PASSES))
             activate(acc, m, s, toks)
 
-        slots = [(0, s, HALF_TOKENS[1]) for s in range(SLICES)]
-        for m in (1, 2):
-            slots += [(m, s, toks) for s in range(SLICES) for toks in HALF_TOKENS]
+        slots = [(m, s, toks) for m in (1, 2) for s in range(SLICES) for toks in HALF_TOKENS]
         chunks = [(m, s) for m in (1, 2, 3) for s in range(SLICES)]
         half_0, half_1 = HALF_TOKENS
 
         def prepare(i):
             if i < len(chunks):
                 regroup(*chunks[i], 0, S)
-                regroup(*chunks[i], 2, S if i in (5, 8) else V)
+                regroup(*chunks[i], 2, S if i in (5, 8, 10) else V)
 
+        prepare(0)
+        prepare(1)
+        quantise(*chunks[0])
         for j in range(len(slots) // 2):
-            prepare(j)
-            if j == 9:
-                prepare(10)
-            if 1 <= j:
-                quantise(*chunks[j - 1])
-            group(*slots[2 * j])
-            if j == 0:
-                for s in range(SLICES):
-                    subtract_query(0, s, half_0)
-            if j == 1 or j == 2:
-                for s in (2 * j - 2, 2 * j - 1):
-                    subtract_query(0, s, half_1)
-            group(*slots[2 * j + 1])
-            if 3 <= j <= 6:
-                weigh(0, j - 3, ALL_TOKENS)
-            if j == 6:
-                transpose_back(0, range(0, 4), range(SLICES), flip_pool, "flip")
+            prepare(j + 2)
             if j == 7:
+                prepare(10)
+                prepare(11)
+            quantise(*chunks[j + 1])
+            group(*slots[2 * j])
+            if j == 0 or j == 1:
+                for s in (2 * j, 2 * j + 1):
+                    subtract_query(0, s, ALL_TOKENS)
+            group(*slots[2 * j + 1])
+            if 1 <= j <= 4:
+                weigh(0, j - 1, ALL_TOKENS)
+            if j == 4:
+                transpose_back(0, range(0, 4), range(SLICES), flip_pool, "flip")
+            if j == 5:
                 add_query_and_store(0, range(0, 4))
                 transpose_back(0, range(4, 8), range(SLICES), flip_pool, "flip")
-            if j == 8:
+            if j == 6:
                 add_query_and_store(0, range(4, 6))
-            if j == 9:
+            if j == 7:
                 add_query_and_store(0, range(6, 8))
                 subtract_query(1, 0, ALL_TOKENS)
         quantise(3, 1)
-        prepare(11)
         group(3, 0, half_0)
         quantise(3, 2)
         group(3, 1, half_0)
         subtract_query(1, 1, ALL_TOKENS)
         quantise(3, 3)
         group(3, 2, half_0)
+        subtract_query(1, 2, ALL_TOKENS)
         weigh(1, 0, half_0)
         weigh(1, 1, half_0)
         group(3, 3, half_0)
-        subtract_query(1, 2, ALL_TOKENS)
-        weigh(1, 2, half_0)
         subtract_query(1, 3, ALL_TOKENS)
+        weigh(1, 2, half_0)
         weigh(1, 3, half_0)
         quarters = (slice(512, 768), slice(768, 1024))
         for part, toks in enumerate(quarters):

@@ -50,6 +50,7 @@ def tile_smcmr_pb_kernel(tc, query, weighted_ctx, W_lin, b_lin, W_gate, b_gate, 
         result_pool = ctx.enter_context(tc.tile_pool(name="result", bufs=4))
         acc_pool = ctx.enter_context(tc.psum_pool(name="acc", bufs=4))
         flip_pool = ctx.enter_context(tc.psum_pool(name="flip", bufs=4))
+        ctx.enter_context(tc.manual_schedule())
 
         q_sb = keep.tile([P, TOKEN_TILES * FEATURES], BF16)
         q_tiles = q_sb[:].rearrange("p (i d) -> p i d", i=TOKEN_TILES)
@@ -75,13 +76,13 @@ def tile_smcmr_pb_kernel(tc, query, weighted_ctx, W_lin, b_lin, W_gate, b_gate, 
             load_tokens(0, first)
         load_tokens(1, 0)
         load_tokens(1, 2)
+        nc.sync.dma_start(out=bias_lin_raw[:], in_=b_lin.rearrange("(b j s) -> j b s", j=P, s=SLICES))
+        nc.sync.dma_start(out=bias_gate_raw[:], in_=b_gate.rearrange("(b j s) -> j b s", j=P, s=SLICES))
         load_weights(0, 0)
         load_tokens(1, 4)
         load_tokens(1, 6)
         for c in range(1, PASSES):
             load_weights(0, c)
-        nc.sync.dma_start(out=bias_lin_raw[:], in_=b_lin.rearrange("(b j s) -> j b s", j=P, s=SLICES))
-        nc.sync.dma_start(out=bias_gate_raw[:], in_=b_gate.rearrange("(b j s) -> j b s", j=P, s=SLICES))
         for m in range(1, STEPS):
             for c in range(PASSES):
                 load_weights(m, c)
@@ -239,37 +240,33 @@ def tile_smcmr_pb_kernel(tc, query, weighted_ctx, W_lin, b_lin, W_gate, b_gate, 
                 nc.sync.dma_start(out=out_dram[:, i, cols], in_=result[:])
 
         S, V = "scalar", "vector"
-        with tc.manual_schedule():
-            for first, engines in ((0, (S, V)), (2, (S, V)), (4, (S, V))):
-                flip_tokens(0, first, engines)
-            quantise_tokens(0, 0)
-            flip_tokens(0, 6, (S, V))
-            quantise_tokens(0, 1)
-            flip_tokens(1, 0, (S, S))
-            flip_tokens(1, 2, (S, S))
-            regroup(0, 0, 0, S)
-            regroup(0, 0, 2, V)
-            quantise_tokens(1, 0)
-            quantise(0, 0)
-            flip_tokens(1, 4, (S, V))
-            flip_tokens(1, 6, (S, V))
-            quantise_tokens(1, 1)
-            for c in range(1, PASSES):
-                regroup(0, c, 0, S)
-                regroup(0, c, 2, V)
-                quantise(0, c)
-            accs = {}
-            for half, (pool, tag) in enumerate(((acc_pool, "acc"), (flip_pool, "flip"))):
-                for s in range(SLICES):
-                    acc = pool.tile([P, HALF], F32, tag=tag, name="acc")
-                    accs[(half, s)] = acc
-            for c in range(PASSES):
-                for half in range(HALVES):
-                    for s in range(SLICES):
-                        multiply(accs[(half, s)], 0, s, HALF_TOKENS[half], (c,))
+        for first, engines in ((0, (S, V)), (2, (S, V)), (4, (S, V))):
+            flip_tokens(0, first, engines)
+        quantise_tokens(0, 0)
+        flip_tokens(0, 6, (S, V))
+        quantise_tokens(0, 1)
+        flip_tokens(1, 0, (S, S))
+        flip_tokens(1, 2, (S, S))
+        regroup(0, 0, 0, S)
+        regroup(0, 0, 2, V)
+        quantise_tokens(1, 0)
+        quantise(0, 0)
+        flip_tokens(1, 4, (S, V))
+        flip_tokens(1, 6, (S, V))
+        quantise_tokens(1, 1)
+        for c in range(1, PASSES):
+            regroup(0, c, 0, S)
+            regroup(0, c, 2, V)
+            quantise(0, c)
+        accs = {}
+        for half, (pool, tag) in enumerate(((acc_pool, "acc"), (flip_pool, "flip"))):
+            for s in range(SLICES):
+                acc = pool.tile([P, HALF], F32, tag=tag, name="acc")
+                accs[(half, s)] = acc
+        for c in range(PASSES):
             for half in range(HALVES):
                 for s in range(SLICES):
-                    activate(accs[(half, s)], 0, s, HALF_TOKENS[half])
+                    multiply(accs[(half, s)], 0, s, HALF_TOKENS[half], (c,))
 
         def group(m, s, toks):
             acc = acc_pool.tile([P, toks.stop - toks.start], F32, tag="acc", name="acc")
@@ -283,58 +280,71 @@ def tile_smcmr_pb_kernel(tc, query, weighted_ctx, W_lin, b_lin, W_gate, b_gate, 
         def prepare(i):
             if i < len(chunks):
                 regroup(*chunks[i], 0, S)
-                regroup(*chunks[i], 2, S if i in (5, 8, 10) else V)
+                regroup(*chunks[i], 2, S if i in (7, 8) else V)
 
         prepare(0)
         prepare(1)
         quantise(*chunks[0])
+        prepare(2)
+        for half in range(HALVES):
+            for s in range(SLICES):
+                activate(accs[(half, s)], 0, s, HALF_TOKENS[half])
+        quantise(*chunks[1])
         for j in range(len(slots) // 2):
-            prepare(j + 2)
+            prepare(j + 3)
             if j == 7:
-                prepare(10)
                 prepare(11)
-            quantise(*chunks[j + 1])
+            if j + 2 < len(chunks):
+                quantise(*chunks[j + 2])
             group(*slots[2 * j])
             if j == 0 or j == 1:
                 for s in (2 * j, 2 * j + 1):
                     subtract_query(0, s, ALL_TOKENS)
+            if j == 5:
+                transpose_back(0, range(0, 4), range(SLICES), flip_pool, "flip")
+            if j == 6:
+                transpose_back(0, range(4, 8), range(SLICES), flip_pool, "flip")
             group(*slots[2 * j + 1])
             if 1 <= j <= 4:
                 weigh(0, j - 1, ALL_TOKENS)
-            if j == 4:
-                transpose_back(0, range(0, 4), range(SLICES), flip_pool, "flip")
             if j == 5:
                 add_query_and_store(0, range(0, 4))
-                transpose_back(0, range(4, 8), range(SLICES), flip_pool, "flip")
             if j == 6:
-                add_query_and_store(0, range(4, 6))
-            if j == 7:
-                add_query_and_store(0, range(6, 8))
-                subtract_query(1, 0, ALL_TOKENS)
-        quantise(3, 1)
+                add_query_and_store(0, range(4, 8))
+            if j >= 5:
+                subtract_query(1, j - 5, ALL_TOKENS)
         group(3, 0, half_0)
         quantise(3, 2)
         group(3, 1, half_0)
-        subtract_query(1, 1, ALL_TOKENS)
+        weigh(1, 0, half_0)
         quantise(3, 3)
         group(3, 2, half_0)
-        subtract_query(1, 2, ALL_TOKENS)
-        weigh(1, 0, half_0)
+        subtract_query(1, 3, ALL_TOKENS)
         weigh(1, 1, half_0)
         group(3, 3, half_0)
-        subtract_query(1, 3, ALL_TOKENS)
         weigh(1, 2, half_0)
-        weigh(1, 3, half_0)
         quarters = (slice(512, 768), slice(768, 1024))
-        for part, toks in enumerate(quarters):
-            for s in range(SLICES):
-                group(3, s, toks)
-                if part == 0 and s == 1:
-                    transpose_back(1, range(0, 4), range(SLICES), flip_pool, "flip")
-                    add_query_and_store(1, range(0, 4))
-                if part == 1 and s == 1:
-                    transpose_back(1, range(4, 6), range(SLICES), flip_pool, "flip")
-                    add_query_and_store(1, range(4, 6))
-                weigh(1, s, toks)
+        group(3, 0, quarters[0])
+        weigh(1, 3, half_0)
+        group(3, 1, quarters[0])
+        weigh(1, 0, quarters[0])
+        group(3, 2, quarters[0])
+        transpose_back(1, range(0, 4), range(SLICES), flip_pool, "flip")
+        weigh(1, 1, quarters[0])
+        group(3, 3, quarters[0])
+        add_query_and_store(1, range(0, 2))
+        weigh(1, 2, quarters[0])
+        group(3, 0, quarters[1])
+        weigh(1, 3, quarters[0])
+        add_query_and_store(1, range(2, 4))
+        group(3, 1, quarters[1])
+        weigh(1, 0, quarters[1])
+        group(3, 2, quarters[1])
+        transpose_back(1, range(4, 6), range(SLICES), flip_pool, "flip")
+        weigh(1, 1, quarters[1])
+        group(3, 3, quarters[1])
+        weigh(1, 2, quarters[1])
+        add_query_and_store(1, range(4, 6))
+        weigh(1, 3, quarters[1])
         transpose_back(1, range(6, 8), range(SLICES), flip_pool, "flip")
         add_query_and_store(1, range(6, 8))

@@ -28,6 +28,7 @@ BLOCK = 512
 BLOCKS = FEATURES // BLOCK
 SLICES = BLOCK // P
 STEPS = 2 * BLOCKS
+PASS_MAJOR = 2
 CHUNK = 4
 
 FLOPS = 2 * TOKENS * 2 * FEATURES * 2 * FEATURES
@@ -72,17 +73,20 @@ def tile_smcmr_pb_kernel(tc, query, weighted_ctx, W_lin, b_lin, W_gate, b_gate, 
             cols = slice((m // 2) * BLOCK, (m // 2 + 1) * BLOCK)
             nc.sync.dma_start(out=raws[m][:, c], in_=w_dram[m % 2][c, :, :, cols])
 
-        for first in range(0, TOKEN_TILES, 2):
-            load_tokens(0, first)
+        load_weights(0, 0)
+        load_tokens(0, 0)
+        load_tokens(0, 2)
+        load_tokens(0, 4)
+        load_weights(0, 1)
+        load_tokens(0, 6)
         load_tokens(1, 0)
         load_tokens(1, 2)
         nc.sync.dma_start(out=bias_lin_raw[:], in_=b_lin.rearrange("(b j s) -> j b s", j=P, s=SLICES))
         nc.sync.dma_start(out=bias_gate_raw[:], in_=b_gate.rearrange("(b j s) -> j b s", j=P, s=SLICES))
-        load_weights(0, 0)
+        load_weights(0, 2)
         load_tokens(1, 4)
         load_tokens(1, 6)
-        for c in range(1, PASSES):
-            load_weights(0, c)
+        load_weights(0, 3)
         for m in range(1, STEPS):
             for c in range(PASSES):
                 load_weights(m, c)
@@ -150,7 +154,7 @@ def tile_smcmr_pb_kernel(tc, query, weighted_ctx, W_lin, b_lin, W_gate, b_gate, 
                 grouped_w[(m, chunk)] = tile
             dst = grouped_w[(m, chunk)][:, first : first + 2].rearrange("p x (a i) t -> p x a t i", i=4)
             values = raws[m][:].rearrange("p c t (j s) -> p c s t j", s=SLICES)
-            if m == 0:
+            if m < PASS_MAJOR:
                 src = values[:, chunk, first : first + 2]
             else:
                 src = values[:, first : first + 2, chunk]
@@ -172,7 +176,7 @@ def tile_smcmr_pb_kernel(tc, query, weighted_ctx, W_lin, b_lin, W_gate, b_gate, 
 
         def multiply(acc, m, s, toks, passes):
             for c in passes:
-                chunk, x = (c, s) if m == 0 else (s, c)
+                chunk, x = (c, s) if m < PASS_MAJOR else (s, c)
                 codes, scales = weights[(m, chunk)]
                 nc.tensor.matmul_mx(
                     out=acc[:],
@@ -240,24 +244,30 @@ def tile_smcmr_pb_kernel(tc, query, weighted_ctx, W_lin, b_lin, W_gate, b_gate, 
                 nc.sync.dma_start(out=out_dram[:, i, cols], in_=result[:])
 
         S, V = "scalar", "vector"
-        for first, engines in ((0, (S, V)), (2, (S, V)), (4, (S, V))):
-            flip_tokens(0, first, engines)
+        regroup(0, 0, 0, V)
+        regroup(0, 0, 2, V)
+        flip_tokens(0, 0, (S, S))
+        flip_tokens(0, 2, (S, S))
+        quantise(0, 0)
+        flip_tokens(0, 4, (S, S))
         quantise_tokens(0, 0)
-        flip_tokens(0, 6, (S, V))
+        regroup(0, 1, 0, V)
+        regroup(0, 1, 2, V)
+        flip_tokens(0, 6, (S, S))
         quantise_tokens(0, 1)
+        quantise(0, 1)
         flip_tokens(1, 0, (S, S))
         flip_tokens(1, 2, (S, S))
-        regroup(0, 0, 0, S)
-        regroup(0, 0, 2, V)
+        regroup(0, 2, 0, V)
+        regroup(0, 2, 2, V)
         quantise_tokens(1, 0)
-        quantise(0, 0)
-        flip_tokens(1, 4, (S, V))
+        quantise(0, 2)
+        flip_tokens(1, 4, (S, S))
         flip_tokens(1, 6, (S, V))
+        regroup(0, 3, 0, S)
+        regroup(0, 3, 2, V)
         quantise_tokens(1, 1)
-        for c in range(1, PASSES):
-            regroup(0, c, 0, S)
-            regroup(0, c, 2, V)
-            quantise(0, c)
+        quantise(0, 3)
         accs = {}
         for half, (pool, tag) in enumerate(((acc_pool, "acc"), (flip_pool, "flip"))):
             for s in range(SLICES):
@@ -274,50 +284,62 @@ def tile_smcmr_pb_kernel(tc, query, weighted_ctx, W_lin, b_lin, W_gate, b_gate, 
             activate(acc, m, s, toks)
 
         slots = [(m, s, toks) for m in (1, 2) for s in range(SLICES) for toks in HALF_TOKENS]
-        chunks = [(m, s) for m in (1, 2, 3) for s in range(SLICES)]
+        chunks = [(m, k) for m in (1, 2, 3) for k in range(CHUNK)]
         half_0, half_1 = HALF_TOKENS
 
         def prepare(i):
-            if i < len(chunks):
-                regroup(*chunks[i], 0, S)
-                regroup(*chunks[i], 2, S if i in (7, 8) else V)
+            regroup(*chunks[i], 0, V if i in () else S)
+            regroup(*chunks[i], 2, S if i in (9, 10, 11) else V)
+
+        def first_products(half):
+            for s in range(SLICES):
+                activate(accs[(half, s)], 0, s, HALF_TOKENS[half])
 
         prepare(0)
         prepare(1)
         quantise(*chunks[0])
         prepare(2)
-        for half in range(HALVES):
-            for s in range(SLICES):
-                activate(accs[(half, s)], 0, s, HALF_TOKENS[half])
         quantise(*chunks[1])
+        prepare(3)
+        quantise(*chunks[2])
+        first_products(0)
+        quantise(*chunks[3])
+        first_products(1)
+        subtract_query(0, 0, half_0)
+        subtract_query(0, 1, half_0)
+
         for j in range(len(slots) // 2):
-            prepare(j + 3)
-            if j == 7:
-                prepare(11)
-            if j + 2 < len(chunks):
-                quantise(*chunks[j + 2])
             group(*slots[2 * j])
-            if j == 0 or j == 1:
-                for s in (2 * j, 2 * j + 1):
-                    subtract_query(0, s, ALL_TOKENS)
-            if j == 5:
-                transpose_back(0, range(0, 4), range(SLICES), flip_pool, "flip")
+            if j == 0:
+                for s in (2, 3):
+                    subtract_query(0, s, half_0)
+                for s in (0, 1):
+                    subtract_query(0, s, half_1)
+            if j == 1:
+                for s in (2, 3):
+                    subtract_query(0, s, half_1)
+            if j + 4 < len(chunks):
+                prepare(j + 4)
+            if j > 0:
+                quantise(*chunks[j + 3])
             if j == 6:
+                transpose_back(0, range(0, 4), range(SLICES), flip_pool, "flip")
+            if j == 7:
                 transpose_back(0, range(4, 8), range(SLICES), flip_pool, "flip")
             group(*slots[2 * j + 1])
             if 1 <= j <= 4:
                 weigh(0, j - 1, ALL_TOKENS)
-            if j == 5:
-                add_query_and_store(0, range(0, 4))
             if j == 6:
+                add_query_and_store(0, range(0, 4))
+            if j == 7:
                 add_query_and_store(0, range(4, 8))
             if j >= 5:
                 subtract_query(1, j - 5, ALL_TOKENS)
+
+        quantise(*chunks[11])
         group(3, 0, half_0)
-        quantise(3, 2)
         group(3, 1, half_0)
         weigh(1, 0, half_0)
-        quantise(3, 3)
         group(3, 2, half_0)
         subtract_query(1, 3, ALL_TOKENS)
         weigh(1, 1, half_0)

@@ -81,12 +81,12 @@ def tile_smcmr_pb_kernel(tc, query, weighted_ctx, W_lin, b_lin, W_gate, b_gate, 
         load_tokens(0, 6)
         load_tokens(1, 0)
         load_tokens(1, 2)
-        nc.sync.dma_start(out=bias_lin_raw[:], in_=b_lin.rearrange("(b j s) -> j b s", j=P, s=SLICES))
-        nc.sync.dma_start(out=bias_gate_raw[:], in_=b_gate.rearrange("(b j s) -> j b s", j=P, s=SLICES))
         load_weights(0, 2)
         load_tokens(1, 4)
         load_tokens(1, 6)
         load_weights(0, 3)
+        nc.sync.dma_start(out=bias_lin_raw[:], in_=b_lin.rearrange("(b j s) -> j b s", j=P, s=SLICES))
+        nc.sync.dma_start(out=bias_gate_raw[:], in_=b_gate.rearrange("(b j s) -> j b s", j=P, s=SLICES))
         for m in range(1, STEPS):
             for c in range(PASSES):
                 load_weights(m, c)
@@ -218,6 +218,13 @@ def tile_smcmr_pb_kernel(tc, query, weighted_ctx, W_lin, b_lin, W_gate, b_gate, 
             mix = mixes[block][:, s, toks]
             nc.vector.tensor_sub(out=mix, in0=mix, in1=grouped_values[:, block, toks, s])
 
+        markers = {U8: keep.tile([P, 1], U8, name="marker_u8"), BF16: keep.tile([P, 1], BF16, name="marker_bf16")}
+
+        def subtract_beside_adds(block, s, column, dtype):
+            mix = mixes[block][:, s, ALL_TOKENS]
+            nc.gpsimd.tensor_copy(out=markers[dtype][:], in_=column)
+            nc.gpsimd.tensor_sub(out=mix, in0=mix, in1=grouped_values[:, block, ALL_TOKENS, s])
+
         def weigh(block, s, toks):
             mix = mixes[block][:, s, toks]
             nc.vector.tensor_mul(out=mix, in0=mix, in1=aways[block][:, s, toks])
@@ -263,7 +270,7 @@ def tile_smcmr_pb_kernel(tc, query, weighted_ctx, W_lin, b_lin, W_gate, b_gate, 
         quantise_tokens(1, 0)
         quantise(0, 2)
         flip_tokens(1, 4, (S, S))
-        flip_tokens(1, 6, (S, V))
+        flip_tokens(1, 6, (S, S))
         regroup(0, 3, 0, S)
         regroup(0, 3, 2, V)
         quantise_tokens(1, 1)
@@ -289,7 +296,7 @@ def tile_smcmr_pb_kernel(tc, query, weighted_ctx, W_lin, b_lin, W_gate, b_gate, 
 
         def prepare(i):
             regroup(*chunks[i], 0, V if i in () else S)
-            regroup(*chunks[i], 2, S if i in (9, 10, 11) else V)
+            regroup(*chunks[i], 2, S if i in (11,) else V)
 
         def first_products(half):
             for s in range(SLICES):
@@ -320,8 +327,6 @@ def tile_smcmr_pb_kernel(tc, query, weighted_ctx, W_lin, b_lin, W_gate, b_gate, 
                     subtract_query(0, s, half_1)
             if j + 4 < len(chunks):
                 prepare(j + 4)
-            if j > 0:
-                quantise(*chunks[j + 3])
             if j == 6:
                 transpose_back(0, range(0, 4), range(SLICES), flip_pool, "flip")
             if j == 7:
@@ -331,10 +336,14 @@ def tile_smcmr_pb_kernel(tc, query, weighted_ctx, W_lin, b_lin, W_gate, b_gate, 
                 weigh(0, j - 1, ALL_TOKENS)
             if j == 6:
                 add_query_and_store(0, range(0, 4))
+                subtract_beside_adds(1, 1, grouped_w[chunks[j + 4]][:, 2, 0, 0:1], BF16)
             if j == 7:
                 add_query_and_store(0, range(4, 8))
-            if j >= 5:
+                subtract_beside_adds(1, 2, weights[chunks[j + 2]][1][:, 0, 0:1], U8)
+            if j >= 5 and j - 5 not in (1, 2):
                 subtract_query(1, j - 5, ALL_TOKENS)
+            if j > 0:
+                quantise(*chunks[j + 3])
 
         quantise(*chunks[11])
         group(3, 0, half_0)

@@ -114,8 +114,8 @@ def tile_smcmr_pb_kernel(tc, query, weighted_ctx, W_lin, b_lin, W_gate, b_gate, 
         grouped = keep.tile([P, PASSES * TOKENS * PACK], BF16, align_bytes=64)
         grouped_values = grouped[:].rearrange("p (c r t) -> p c r t", c=PASSES, t=PACK)
         grouped_words = grouped[:].bitcast(F32).rearrange("p (c r u) -> p c r u", c=PASSES, u=2)
-        cat_codes = keep.tile([P, PASSES, TOKENS], U32, align_bytes=64)
-        cat_scales = keep.tile([P, PASSES, TOKENS], U8, align_bytes=64)
+        cat_codes = keep.tile([P, PASSES, TOKENS], U32, align_bytes=256)
+        cat_scales = keep.tile([P, PASSES, TOKENS], U8, align_bytes=256)
 
         def flip_tokens(source, first, engines):
             for g in range(QUERY_PASSES):
@@ -165,8 +165,8 @@ def tile_smcmr_pb_kernel(tc, query, weighted_ctx, W_lin, b_lin, W_gate, b_gate, 
                 nc.vector.tensor_copy(out=dst, in_=src)
 
         def quantise(m, chunk):
-            codes = weight_pool.tile([P, CHUNK, P], U32, align_bytes=64, tag="codes")
-            scales = weight_pool.tile([P, CHUNK, P], U8, align_bytes=64, tag="scales")
+            codes = weight_pool.tile([P, CHUNK, P], U32, align_bytes=256, tag="codes")
+            scales = weight_pool.tile([P, CHUNK, P], U8, align_bytes=256, tag="scales")
             weights[(m, chunk)] = (codes, scales)
             nc.vector.quantize_mx(
                 out=codes[:].rearrange("p x n -> p (x n)").bitcast(FP8X4),

from contextlib import ExitStack

import concourse.masks as masks
import concourse.mybir as mybir

FP8X4 = mybir.dt.float8_e4m3fn_x4
BF16 = mybir.dt.bfloat16
F32 = mybir.dt.float32
U32 = mybir.dt.uint32
U8 = mybir.dt.uint8
ACT = mybir.ActivationFunctionType
ALU = mybir.AluOpType

P = 128
PACK = 4
K_PASS = P * PACK
TOKENS = 1024
FEATURES = 1024
PASSES = 2 * FEATURES // K_PASS
QUERY_PASSES = FEATURES // K_PASS
TOKEN_TILES = TOKENS // P
HALF = 512
HALVES = TOKENS // HALF
TILES_PER_HALF = HALF // P
HALF_TOKENS = [slice(h * HALF, (h + 1) * HALF) for h in range(HALVES)]
ALL_TOKENS = slice(0, TOKENS)
BLOCK = 512
BLOCKS = FEATURES // BLOCK
SLICES = BLOCK // P
STEPS = 2 * BLOCKS
PASS_MAJOR = 2
CHUNK = 4

FLOPS = 2 * TOKENS * 2 * FEATURES * 2 * FEATURES


def tile_smcmr_pb_kernel(tc, query, weighted_ctx, W_lin, b_lin, W_gate, b_gate, out):
    nc = tc.nc
    q_dram = query.flatten_outer_dims().rearrange("(p i) d -> p i d", i=TOKEN_TILES)
    c_dram = weighted_ctx.flatten_outer_dims().rearrange("(p i) d -> p i d", i=TOKEN_TILES)
    out_dram = out.flatten_outer_dims().rearrange("(p i) d -> p i d", i=TOKEN_TILES)
    w_dram = [w.rearrange("(c p t) n -> c p t n", p=P, t=PACK) for w in (W_lin, W_gate)]

    with ExitStack() as ctx:
        keep = ctx.enter_context(tc.tile_pool(name="keep", bufs=1))
        raw_pool = ctx.enter_context(tc.tile_pool(name="raw", bufs=3))
        grouped_pool = ctx.enter_context(tc.tile_pool(name="grouped", bufs=4))
        weight_pool = ctx.enter_context(tc.tile_pool(name="weights", bufs=8))
        hidden_pool = ctx.enter_context(tc.tile_pool(name="hidden", bufs=2))
        gate_pool = ctx.enter_context(tc.tile_pool(name="gate", bufs=1))
        result_pool = ctx.enter_context(tc.tile_pool(name="result", bufs=4))
        acc_pool = ctx.enter_context(tc.psum_pool(name="acc", bufs=4))
        flip_pool = ctx.enter_context(tc.psum_pool(name="flip", bufs=4))
        ctx.enter_context(tc.manual_schedule())

        q_sb = keep.tile([P, TOKEN_TILES * FEATURES], BF16)
        q_tiles = q_sb[:].rearrange("p (i d) -> p i d", i=TOKEN_TILES)
        c_sb = keep.tile([P, TOKEN_TILES * FEATURES], BF16)
        c_tiles = c_sb[:].rearrange("p (i d) -> p i d", i=TOKEN_TILES)
        words = [q_sb[:].bitcast(F32), c_sb[:].bitcast(F32)]
        bias_lin_raw = keep.tile([P, BLOCKS, SLICES], BF16)
        bias_gate_raw = keep.tile([P, BLOCKS, SLICES], BF16)
        raws = []

        def load_tokens(source, first):
            tiles, dram = ((q_tiles, q_dram), (c_tiles, c_dram))[source]
            nc.sync.dma_start(out=tiles[:, first : first + 2, :], in_=dram[:, first : first + 2, :])

        def load_weights(m, c):
            if len(raws) == m:
                raw = raw_pool.tile([P, PASSES, PACK, BLOCK], BF16, tag="raw", name="raw%d" % m)
                raws.append(raw)
            cols = slice((m // 2) * BLOCK, (m // 2 + 1) * BLOCK)
            nc.sync.dma_start(out=raws[m][:, c], in_=w_dram[m % 2][c, :, :, cols])

        load_weights(0, 0)
        load_tokens(0, 0)
        load_tokens(0, 2)
        load_tokens(0, 4)
        load_weights(0, 1)
        load_tokens(0, 6)
        load_tokens(1, 0)
        load_tokens(1, 2)
        load_weights(0, 2)
        load_tokens(1, 4)
        load_tokens(1, 6)
        load_weights(0, 3)
        nc.sync.dma_start(out=bias_lin_raw[:], in_=b_lin.rearrange("(b j s) -> j b s", j=P, s=SLICES))
        nc.sync.dma_start(out=bias_gate_raw[:], in_=b_gate.rearrange("(b j s) -> j b s", j=P, s=SLICES))
        for m in range(1, STEPS):
            for c in range(PASSES):
                load_weights(m, c)

        ident_f32 = keep.tile([P, P], F32)
        masks.make_identity(nc, ident_f32[:])

        warm_in = keep.tile([P, 1], F32)
        warm_out = keep.tile([P, 1], F32)
        nc.vector.memset(warm_in[:], 0.0)
        nc.scalar.activation(out=warm_out[:], in_=warm_in[:], func=ACT.Sigmoid)

        bias_lin = keep.tile([P, BLOCKS * SLICES], F32)
        neg_bias_gate = keep.tile([P, BLOCKS * SLICES], F32)
        nc.gpsimd.tensor_copy(out=bias_lin[:], in_=bias_lin_raw[:].rearrange("p b s -> p (b s)"))
        nc.gpsimd.tensor_scalar(
            out=neg_bias_gate[:],
            in0=bias_gate_raw[:].rearrange("p b s -> p (b s)"),
            scalar1=-1.0,
            scalar2=0.0,
            op0=ALU.mult,
            op1=ALU.add,
        )

        grouped = keep.tile([P, PASSES * TOKENS * PACK], BF16, align_bytes=64)
        grouped_values = grouped[:].rearrange("p (c r t) -> p c r t", c=PASSES, t=PACK)
        grouped_words = grouped[:].bitcast(F32).rearrange("p (c r u) -> p c r u", c=PASSES, u=2)
        cat_codes = keep.tile([P, PASSES, TOKENS], U32, align_bytes=256)
        cat_scales = keep.tile([P, PASSES, TOKENS], U8, align_bytes=256)

        def flip_tokens(source, first, engines):
            for g in range(QUERY_PASSES):
                c = source * QUERY_PASSES + g
                flipped = flip_pool.tile([P, 2, 2, P], F32, tag="flip")
                for a in range(2):
                    for u in range(2):
                        w0 = (first + a) * (FEATURES // 2) + g * (K_PASS // 2)
                        nc.tensor.transpose(
                            flipped[:, a, u, :], words[source][:, w0 + u : w0 + 2 * P : 2], ident_f32[:]
                        )
                dst = grouped_words[:, c, first * P : (first + 2) * P, :].rearrange("p (a r) u -> p a r u", a=2)
                src = flipped[:].rearrange("p a u r -> p a r u")
                if engines[g] == "scalar":
                    nc.scalar.copy(out=dst, in_=src)
                else:
                    nc.vector.tensor_copy(out=dst, in_=src)

        def quantise_tokens(source, half):
            toks = slice(half * HALF, (half + 1) * HALF)
            for g in range(QUERY_PASSES):
                c = source * QUERY_PASSES + g
                start = (c * TOKENS + half * HALF) * PACK
                nc.vector.quantize_mx(
                    out=cat_codes[:, c, toks].bitcast(FP8X4),
                    scales=cat_scales[:, c, toks],
                    in_=grouped[:, start : start + HALF * PACK],
                )

        grouped_w = {}
        weights = {}

        def regroup(m, chunk, first, engine):
            if (m, chunk) not in grouped_w:
                tile = grouped_pool.tile([P, CHUNK, P, PACK], BF16, align_bytes=64, tag="grouped_w")
                grouped_w[(m, chunk)] = tile
            dst = grouped_w[(m, chunk)][:, first : first + 2].rearrange("p x (a i) t -> p x a t i", i=4)
            values = raws[m][:].rearrange("p c t (j s) -> p c s t j", s=SLICES)
            if m < PASS_MAJOR:
                src = values[:, chunk, first : first + 2]
            else:
                src = values[:, first : first + 2, chunk]
            src = src.rearrange("p x t (a i) -> p x a t i", i=4)
            if engine == "scalar":
                nc.scalar.copy(out=dst, in_=src)
            else:
                nc.vector.tensor_copy(out=dst, in_=src)

        def quantise(m, chunk):
            codes = weight_pool.tile([P, CHUNK, P], U32, align_bytes=256, tag="codes")
            scales = weight_pool.tile([P, CHUNK, P], U8, align_bytes=256, tag="scales")
            weights[(m, chunk)] = (codes, scales)
            nc.vector.quantize_mx(
                out=codes[:].rearrange("p x n -> p (x n)").bitcast(FP8X4),
                scales=scales[:].rearrange("p x n -> p (x n)"),
                in_=grouped_w[(m, chunk)][:].rearrange("p x j t -> p (x j t)"),
            )

        def multiply(acc, m, s, toks, passes):
            for c in passes:
                chunk, x = (c, s) if m < PASS_MAJOR else (s, c)
                codes, scales = weights[(m, chunk)]
                nc.tensor.matmul_mx(
                    out=acc[:],
                    lhsT=codes[:, x, :].bitcast(FP8X4),
                    lhsT_scale=scales[:, x, :],
                    rhs=cat_codes[:, c, toks].bitcast(FP8X4),
                    rhs_scale=cat_scales[:, c, toks],
                    start=(c == 0),
                    stop=(c == PASSES - 1),
                )

        mixes = {}
        aways = {}
        backs = {}

        def activate(acc, m, s, toks):
            block = m // 2
            n = block * SLICES + s
            if m % 2 == 0:
                if block not in mixes:
                    mix = hidden_pool.tile([P, SLICES, TOKENS], F32, tag="mix")
                    mixes[block] = mix
                nc.scalar.activation(
                    out=mixes[block][:, s, toks], in_=acc[:], func=ACT.Tanh, bias=bias_lin[:, n : n + 1], scale=1.0
                )
            else:
                if block not in aways:
                    away = gate_pool.tile([P, SLICES, TOKENS], F32, tag="away")
                    aways[block] = away
                nc.scalar.activation(
                    out=aways[block][:, s, toks],
                    in_=acc[:],
                    func=ACT.Sigmoid,
                    bias=neg_bias_gate[:, n : n + 1],
                    scale=-1.0,
                )

        def subtract_query(block, s, toks):
            mix = mixes[block][:, s, toks]
            nc.vector.tensor_sub(out=mix, in0=mix, in1=grouped_values[:, block, toks, s])

        markers = {U8: keep.tile([P, 1], U8, name="marker_u8"), BF16: keep.tile([P, 1], BF16, name="marker_bf16")}

        def subtract_beside_adds(block, s, column, dtype):
            mix = mixes[block][:, s, ALL_TOKENS]
            nc.gpsimd.tensor_copy(out=markers[dtype][:], in_=column)
            nc.gpsimd.tensor_sub(out=mix, in0=mix, in1=grouped_values[:, block, ALL_TOKENS, s])

        def weigh(block, s, toks):
            mix = mixes[block][:, s, toks]
            nc.vector.tensor_mul(out=mix, in0=mix, in1=aways[block][:, s, toks])

        def transpose_back(block, tiles, slices, pool, tag):
            for i in tiles:
                if (block, i) not in backs:
                    back = pool.tile([P, SLICES, P], F32, tag=tag, name="back")
                    backs[(block, i)] = back
                for s in slices:
                    nc.tensor.transpose(
                        backs[(block, i)][:, s, :], mixes[block][:, s, i * P : (i + 1) * P], ident_f32[:]
                    )

        def add_query_and_store(block, tiles):
            cols = slice(block * BLOCK, (block + 1) * BLOCK)
            for i in tiles:
                result = result_pool.tile([P, BLOCK], F32, tag="result")
                nc.vector.tensor_add(
                    out=result[:].rearrange("p (j s) -> p j s", s=SLICES),
                    in0=backs[(block, i)][:].rearrange("p s j -> p j s"),
                    in1=q_tiles[:, i, cols].rearrange("p (j s) -> p j s", s=SLICES),
                )
                nc.sync.dma_start(out=out_dram[:, i, cols], in_=result[:])

        S, V = "scalar", "vector"
        regroup(0, 0, 0, V)
        regroup(0, 0, 2, V)
        flip_tokens(0, 0, (S, S))
        flip_tokens(0, 2, (S, S))
        quantise(0, 0)
        flip_tokens(0, 4, (S, S))
        quantise_tokens(0, 0)
        regroup(0, 1, 0, V)
        regroup(0, 1, 2, V)
        flip_tokens(0, 6, (S, S))
        quantise_tokens(0, 1)
        quantise(0, 1)
        flip_tokens(1, 0, (S, S))
        flip_tokens(1, 2, (S, S))
        regroup(0, 2, 0, V)
        regroup(0, 2, 2, V)
        quantise_tokens(1, 0)
        quantise(0, 2)
        flip_tokens(1, 4, (S, S))
        flip_tokens(1, 6, (S, S))
        regroup(0, 3, 0, S)
        regroup(0, 3, 2, V)
        quantise_tokens(1, 1)
        quantise(0, 3)
        accs = {}
        for half, (pool, tag) in enumerate(((acc_pool, "acc"), (flip_pool, "flip"))):
            for s in range(SLICES):
                acc = pool.tile([P, HALF], F32, tag=tag, name="acc")
                accs[(half, s)] = acc
        for c in range(PASSES):
            for half in range(HALVES):
                for s in range(SLICES):
                    multiply(accs[(half, s)], 0, s, HALF_TOKENS[half], (c,))

        def group(m, s, toks):
            acc = acc_pool.tile([P, toks.stop - toks.start], F32, tag="acc", name="acc")
            multiply(acc, m, s, toks, range(PASSES))
            activate(acc, m, s, toks)

        slots = [(m, s, toks) for m in (1, 2) for s in range(SLICES) for toks in HALF_TOKENS]
        chunks = [(m, k) for m in (1, 2, 3) for k in range(CHUNK)]
        half_0, half_1 = HALF_TOKENS

        def prepare(i):
            regroup(*chunks[i], 0, V if i in () else S)
            regroup(*chunks[i], 2, S if i in (11,) else V)

        def first_products(half):
            for s in range(SLICES):
                activate(accs[(half, s)], 0, s, HALF_TOKENS[half])

        prepare(0)
        prepare(1)
        quantise(*chunks[0])
        prepare(2)
        quantise(*chunks[1])
        prepare(3)
        quantise(*chunks[2])
        first_products(0)
        quantise(*chunks[3])
        first_products(1)
        subtract_query(0, 0, half_0)
        subtract_query(0, 1, half_0)

        for j in range(len(slots) // 2):
            group(*slots[2 * j])
            if j == 0:
                for s in (2, 3):
                    subtract_query(0, s, half_0)
                for s in (0, 1):
                    subtract_query(0, s, half_1)
            if j == 1:
                for s in (2, 3):
                    subtract_query(0, s, half_1)
            if j + 4 < len(chunks):
                prepare(j + 4)
            if j == 6:
                transpose_back(0, range(0, 4), range(SLICES), flip_pool, "flip")
            if j == 7:
                transpose_back(0, range(4, 8), range(SLICES), flip_pool, "flip")
            group(*slots[2 * j + 1])
            if 1 <= j <= 4:
                weigh(0, j - 1, ALL_TOKENS)
            if j == 6:
                add_query_and_store(0, range(0, 4))
                subtract_beside_adds(1, 1, grouped_w[chunks[j + 4]][:, 2, 0, 0:1], BF16)
            if j == 7:
                add_query_and_store(0, range(4, 8))
                subtract_beside_adds(1, 2, weights[chunks[j + 2]][1][:, 0, 0:1], U8)
            if j >= 5 and j - 5 not in (1, 2):
                subtract_query(1, j - 5, ALL_TOKENS)
            if j > 0:
                quantise(*chunks[j + 3])

        quantise(*chunks[11])
        group(3, 0, half_0)
        group(3, 1, half_0)
        weigh(1, 0, half_0)
        group(3, 2, half_0)
        subtract_query(1, 3, ALL_TOKENS)
        weigh(1, 1, half_0)
        group(3, 3, half_0)
        weigh(1, 2, half_0)
        quarters = (slice(512, 768), slice(768, 1024))
        group(3, 0, quarters[0])
        weigh(1, 3, half_0)
        group(3, 1, quarters[0])
        weigh(1, 0, quarters[0])
        group(3, 2, quarters[0])
        transpose_back(1, range(0, 4), range(SLICES), flip_pool, "flip")
        weigh(1, 1, quarters[0])
        group(3, 3, quarters[0])
        add_query_and_store(1, range(0, 2))
        weigh(1, 2, quarters[0])
        group(3, 0, quarters[1])
        weigh(1, 3, quarters[0])
        add_query_and_store(1, range(2, 4))
        group(3, 1, quarters[1])
        weigh(1, 0, quarters[1])
        group(3, 2, quarters[1])
        transpose_back(1, range(4, 6), range(SLICES), flip_pool, "flip")
        weigh(1, 1, quarters[1])
        group(3, 3, quarters[1])
        weigh(1, 2, quarters[1])
        add_query_and_store(1, range(4, 6))
        weigh(1, 3, quarters[1])
        transpose_back(1, range(6, 8), range(SLICES), flip_pool, "flip")
        add_query_and_store(1, range(6, 8))
